import numpy as np
import ml_dtypes


BF16 = ml_dtypes.bfloat16


def bf(x):
    return np.asarray(x, np.float32).astype(BF16)


def f64(x):
    return np.asarray(x).astype(np.float64)


E2M1 = np.array([0.0, 0.5, 1.0, 1.5, 2.0, 3.0, 4.0, 6.0, -0.0, -0.5, -1.0, -1.5, -2.0, -3.0, -4.0, -6.0])


def pack_weight(w, fmt):
    k, n = w.shape
    w = f64(bf(w)).reshape(k // 32, 32, n)
    amax = np.abs(w).max(1)
    if fmt == "e4m3":
        byte = np.frexp(amax)[1] - 1 + 127 - 7
    else:
        mant, ex = np.frexp(amax / 6.0)
        byte = np.where(mant > 0.5, ex, ex - 1) + 127
    byte = np.clip(np.where(amax > 0, byte, 1), 1, 254)
    scaled = (w * np.exp2(127.0 - byte)[:, None, :]).reshape(k, n).astype(np.float32)
    by_word = np.ascontiguousarray(scaled.reshape(k // 512, 128, 4, n).transpose(0, 1, 3, 2))
    if fmt == "e4m3":
        words = by_word.astype(ml_dtypes.float8_e4m3fn).view(np.uint8)
    else:
        c = by_word.astype(ml_dtypes.float4_e2m1fn).view(np.uint8) & 0xF
        words = c[..., 0::2] | (c[..., 1::2] << 4)
    return np.ascontiguousarray(words), np.ascontiguousarray(byte.astype(np.uint8).reshape(k // 512, 16, n))


def unpack_weight(words, scales, fmt):
    g, p, n, _ = words.shape
    if fmt == "e4m3":
        vals = np.ascontiguousarray(words).view(ml_dtypes.float8_e4m3fn).astype(np.float64)
    else:
        nib = np.empty((g, p, n, 4), np.uint8)
        nib[..., 0::2] = words & 0xF
        nib[..., 1::2] = words >> 4
        vals = E2M1[nib]
    vals = vals * np.repeat(np.exp2(scales.astype(np.float64) - 127.0), 8, axis=1)[..., None]
    return vals.transpose(0, 1, 3, 2).reshape(g * 512, n)

def pack4(w):
    words, scales = pack_weight(w, "e2m1")
    return words.reshape(words.shape[0], 128, -1), scales


def unpack4(words, scales):
    return unpack_weight(words.reshape(words.shape[0], 128, -1, 2), scales, "e2m1")


def kspread(k):
    return np.exp2(np.repeat(np.random.randint(-6, 7, k // 32), 32).astype(np.float64))


B, T, C, H, D = 1, 384, 3072, 16, 128
HD = H * D
HALF = D // 2
EPS = 1.1920928955078125e-07


def rope(u, cos, sin):
    u1, u2 = u[..., :HALF], u[..., HALF:]
    return np.concatenate([u1 * cos + u2 * sin, -u1 * sin + u2 * cos], axis=-1)


def rmsnorm(u):
    return u * (1.0 / np.sqrt(np.mean(u * u, axis=-1, keepdims=True) + EPS))


def setup_inputs():
    s = kspread(C)
    ang = np.arange(T)[:, None] * 10000.0 ** (-np.arange(HALF) / HALF)
    x = np.random.standard_normal((B, T, C)) * s
    wq = np.random.standard_normal((HD, C)) / np.sqrt(C) / s[None, :]
    wk = np.random.standard_normal((HD, C)) / np.sqrt(C) / s[None, :]
    x_words, x_scales = pack4(x.reshape(B * T, C).T)
    wq_words, wq_scales = pack4(wq.T)
    wk_words, wk_scales = pack4(wk.T)
    return {
        "x_words": x_words,
        "x_scales": x_scales,
        "wq_words": wq_words,
        "wq_scales": wq_scales,
        "wk_words": wk_words,
        "wk_scales": wk_scales,
        "cos": bf(np.cos(ang))[None, :, None, :],
        "sin": bf(np.sin(ang))[None, :, None, :],
    }


def reference(x_words, x_scales, wq_words, wq_scales, wk_words, wk_scales, cos, sin):
    xq = unpack4(x_words, x_scales).T.reshape(B, T, C)
    q = (xq @ unpack4(wq_words, wq_scales)).reshape(B, T, H, D)
    k = (xq @ unpack4(wk_words, wk_scales)).reshape(B, T, H, D)
    q = rmsnorm(rope(q, f64(cos), f64(sin)))
    k = rmsnorm(rope(k, f64(cos), f64(sin)))
    return q, k

@@ -1,0 +1,210 @@
+from contextlib import ExitStack
+
+import concourse.mybir as mybir
+
+F32 = mybir.dt.float32
+BF16 = mybir.dt.bfloat16
+I32 = mybir.dt.int32
+U8 = mybir.dt.uint8
+FP4X4 = mybir.dt.float4_e2m1fn_x4
+ACT = mybir.ActivationFunctionType
+ALU = mybir.AluOpType
+
+P = 128
+TOKENS, FEATURES, HEADS, HEAD = 384, 3072, 16, 128
+HALF = HEAD // 2
+EPS = 1.1920928955078125e-07
+PASSES = FEATURES // 512
+TILES = TOKENS // P
+BLOCK = 512
+COLS = HEADS * HEAD
+FLOPS = 2 * TOKENS * FEATURES * 2 * COLS
+
+
+def tile_selfattention_pa_kernel(tc, x_words, x_scales, wq_words, wq_scales, wk_words, wk_scales, cos, sin, out_0, out_1):
+    nc = tc.nc
+    outs = [o.rearrange("b t h d -> (b t) (h d)") for o in (out_0, out_1)]
+    words = (wq_words, wk_words)
+    scales = (wq_scales, wk_scales)
+
+    with ExitStack() as ctx:
+        keep = ctx.enter_context(tc.tile_pool(name="keep", bufs=1))
+        work = ctx.enter_context(tc.tile_pool(name="work", bufs=4))
+        psum = ctx.enter_context(tc.psum_pool(name="psum", bufs=8))
+        ctx.enter_context(tc.manual_schedule())
+
+        def load_planes(plane, src, col0, width):
+            for q in range(4):
+                nc.sync.dma_start(
+                    out=plane[32 * q : 32 * q + 4, :, :].bitcast(I32),
+                    in_=src[:, 4 * q : 4 * q + 4, col0 : col0 + width].rearrange("g r n -> r g n").bitcast(I32),
+                )
+
+        def flat32(plane):
+            return plane[:].rearrange("p g n -> p (g n)").bitcast(I32)
+
+        x_first = keep.tile([P, 1, 2 * TOKENS], U8, align_bytes=64, name="x_first")
+        x_mid = keep.tile([P, 2, 2 * TOKENS], U8, align_bytes=64, name="x_mid")
+        x_last = keep.tile([P, 3, 2 * TOKENS], U8, align_bytes=64, name="x_last")
+        w_first = keep.tile([P, 1, 2 * BLOCK], U8, align_bytes=64, name="w_first")
+        w_mid = keep.tile([P, 2, 2 * BLOCK], U8, align_bytes=64, name="w_mid")
+        w_last = keep.tile([P, 3, 2 * BLOCK], U8, align_bytes=64, name="w_last")
+        x_plane = keep.tile([P, PASSES, TOKENS], U8, align_bytes=64, name="x_plane")
+        plane_q0 = keep.tile([P, PASSES, BLOCK], U8, align_bytes=64, name="plane_q0")
+        plane_q1 = keep.tile([P, PASSES, 3 * BLOCK], U8, align_bytes=64, name="plane_q1")
+        plane_k = keep.tile([P, PASSES, 4 * BLOCK], U8, align_bytes=64, name="plane_k")
+        w_codes = []
+        for b in range(1, 8):
+            wt = keep.tile([P, PASSES, 2 * BLOCK], U8, align_bytes=64, name="w_block%d" % b)
+            w_codes.append(wt)
+
+        zeros = keep.tile([P, BLOCK], BF16, align_bytes=64, name="zeros")
+        nc.vector.memset(zeros[:], 0.0)
+        nc.gpsimd.memset(flat32(x_plane), 0)
+        nc.vector.memset(flat32(plane_q0), 0)
+        nc.vector.memset(flat32(plane_q1), 0)
+        nc.vector.memset(flat32(plane_k), 0)
+
+        def x_src(g0, n):
+            return x_words[g0 : g0 + n, :, :].rearrange("g p n -> p g n")
+
+        def w_src(b, g0, n):
+            c0 = (b % 4) * 2 * BLOCK
+            return words[b // 4][g0 : g0 + n, :, c0 : c0 + 2 * BLOCK].rearrange("g p n -> p g n")
+
+        nc.sync.dma_start(out=w_first[:], in_=w_src(0, 0, 1))
+        nc.sync.dma_start(out=x_first[:], in_=x_src(0, 1))
+        load_planes(x_plane, x_scales, 0, TOKENS)
+        load_planes(plane_q0, scales[0], 0, BLOCK)
+        nc.sync.dma_start(out=w_mid[:], in_=w_src(0, 1, 2))
+        nc.sync.dma_start(out=x_mid[:], in_=x_src(1, 2))
+        nc.sync.dma_start(out=w_last[:], in_=w_src(0, 3, 3))
+        nc.sync.dma_start(out=x_last[:], in_=x_src(3, 3))
+        nc.sync.dma_start(out=w_codes[0][:], in_=w_src(1, 0, 6))
+        load_planes(plane_q1, scales[0], BLOCK, 3 * BLOCK)
+        nc.sync.dma_start(out=w_codes[1][:], in_=w_src(2, 0, 6))
+        nc.sync.dma_start(out=w_codes[2][:], in_=w_src(3, 0, 6))
+        load_planes(plane_k, scales[1], 0, 4 * BLOCK)
+        for b in range(4, 8):
+            nc.sync.dma_start(out=w_codes[b - 1][:], in_=w_src(b, 0, 6))
+
+        cos_sb = keep.tile([P, TILES, HALF], BF16, name="cos_sb")
+        sin_sb = keep.tile([P, TILES, HALF], BF16, name="sin_sb")
+        table = keep.tile([P, TILES, 2, HEAD], BF16, name="table")
+        dummy = keep.tile([P, 1], F32, name="dummy")
+        nc.gpsimd.dma_start(out=cos_sb[:], in_=cos.rearrange("a (t p) b j -> p (a t) (b j)", p=P))
+        nc.gpsimd.dma_start(out=sin_sb[:], in_=sin.rearrange("a (t p) b j -> p (a t) (b j)", p=P))
+        nc.vector.memset(dummy[:], 1.0)
+        nc.scalar.activation(out=dummy[:], in_=dummy[:], func=ACT.Abs_reciprocal_sqrt)
+        nc.scalar.copy(out=table[:, :, 0, 0:HALF], in_=cos_sb[:])
+        nc.scalar.copy(out=table[:, :, 1, HALF:HEAD], in_=cos_sb[:])
+        nc.scalar.copy(out=table[:, :, 0, HALF:HEAD], in_=sin_sb[:])
+        nc.scalar.activation(out=table[:, :, 1, 0:HALF], in_=sin_sb[:], func=ACT.Copy, scale=-1.0)
+
+        def x_pass(g, t):
+            part, i = ((x_first, 0), (x_mid, g - 1), (x_mid, g - 1), (x_last, g - 3), (x_last, g - 3), (x_last, g - 3))[g]
+            return part[:, i, 2 * P * t : 2 * P * (t + 1)]
+
+        def w_pass(b, g, c0, width):
+            if b == 0:
+                part, i = ((w_first, 0), (w_mid, g - 1), (w_mid, g - 1), (w_last, g - 3), (w_last, g - 3), (w_last, g - 3))[g]
+            else:
+                part, i = w_codes[b - 1], g
+            return part[:, i, 2 * c0 : 2 * (c0 + width)]
+
+        def w_scale(b, g, c0, width):
+            if b == 0:
+                return plane_q0[:, g, c0 : c0 + width]
+            if b < 4:
+                c0 = c0 + (b - 1) * BLOCK
+                return plane_q1[:, g, c0 : c0 + width]
+            c0 = c0 + (b - 4) * BLOCK
+            return plane_k[:, g, c0 : c0 + width]
+
+        def mx(acc, b, t, g, c0, width):
+            nc.tensor.matmul_mx(
+                out=acc[:, 0:width],
+                lhsT=x_pass(g, t).bitcast(FP4X4),
+                lhsT_scale=x_plane[:, g, P * t : P * (t + 1)],
+                rhs=w_pass(b, g, c0, width).bitcast(FP4X4),
+                rhs_scale=w_scale(b, g, c0, width),
+                start=(g == 0),
+                stop=(g == PASSES - 1),
+            )
+
+        pieces = [(b, t, 0, BLOCK) for b in range(8) for t in range(TILES)]
+        pieces[-2:] = [(7, 1, 0, 256), (7, 1, 256, 256), (7, 2, 0, 256), (7, 2, 256, 128), (7, 2, 384, 128)]
+
+        def scale_and_store(state):
+            (b, t, c0, width), v, r = state
+            o = work.tile([P, BLOCK], F32, name="o", bufs=8)
+            for h in range(width // HEAD):
+                nc.scalar.activation(out=o[:, h * HEAD : (h + 1) * HEAD], in_=v[:, h * HEAD : (h + 1) * HEAD], func=ACT.Copy, scale=r[:, h : h + 1])
+            col = (b % 4) * BLOCK + c0
+            nc.sync.dma_start(out=outs[b // 4][P * t : P * (t + 1), col : col + width], in_=o[:, 0:width])
+
+        warm = psum.tile([P, BLOCK], F32, name="acc")
+        for i in range(8):
+            nc.tensor.matmul(warm[:], zeros[:, 0:P], zeros[:], start=True, stop=True)
+
+        first = [psum.tile([P, BLOCK], F32, name="acc") for t in range(TILES)]
+        for g in range(PASSES):
+            for t in range(TILES):
+                mx(first[t], 0, t, g, 0, BLOCK)
+
+        def multiply(i):
+            b, t, c0, width = pieces[i]
+            nh = width // HEAD
+            if i < TILES:
+                acc = first[i]
+            else:
+                acc = psum.tile([P, BLOCK], F32, name="acc")
+                for g in range(PASSES):
+                    mx(acc, b, t, g, c0, width)
+            prod = work.tile([P, BLOCK // HEAD, 2, HEAD], F32, name="prod")
+            nc.vector.tensor_tensor(
+                out=prod[:, 0:nh, :, :],
+                in0=acc[:, 0:width].rearrange("p (h d) -> p h d", d=HEAD).unsqueeze(2).to_broadcast([P, nh, 2, HEAD]),
+                in1=table[:, t, :, :].unsqueeze(1).to_broadcast([P, nh, 2, HEAD]),
+                op=ALU.mult,
+            )
+            return prod
+
+        def add(i, prod):
+            width = pieces[i][3]
+            v = work.tile([P, BLOCK], F32, name="v")
+            eng = nc.vector if width == HEAD else nc.gpsimd
+            halves = prod[:, 0 : width // HEAD, :, :].rearrange("p h q d -> p (h q) d")
+            eng.tensor_tensor(
+                out=v[:, 0:width].rearrange("p (m j) -> p m j", j=HALF),
+                in0=halves[:, :, 0:HALF],
+                in1=halves[:, :, HALF:HEAD],
+                op=ALU.add,
+            )
+            return v
+
+        def squares(i, v):
+            ss = work.tile([P, BLOCK // HEAD], F32, name="ss")
+            for h in range(pieces[i][3] // HEAD):
+                sq = work.tile([P, HEAD], F32, name="sq")
+                nc.scalar.activation(out=sq[:], in_=v[:, h * HEAD : (h + 1) * HEAD], func=ACT.Square, accum_out=ss[:, h : h + 1])
+            return ss
+
+        def root(i, ss):
+            nh = pieces[i][3] // HEAD
+            r = work.tile([P, BLOCK // HEAD], F32, name="r")
+            nc.scalar.activation(out=r[:, 0:nh], in_=ss[:, 0:nh], func=ACT.Abs_reciprocal_sqrt, scale=1.0 / HEAD, bias=EPS)
+            return r
+
+        n = len(pieces)
+        prods, vs, rs = {}, {}, {}
+        for i in range(n + 2):
+            if i < n:
+                prods[i] = multiply(i)
+            if 1 <= i <= n:
+                vs[i - 1] = add(i - 1, prods[i - 1])
+                ss = squares(i - 1, vs[i - 1])
+            if i >= 2:
+                scale_and_store((pieces[i - 2], vs[i - 2], rs[i - 2]))
+            if 1 <= i <= n:
+                rs[i - 1] = root(i - 1, ss)

@@ -54,8 +54,8 @@ def tile_selfattention_pa_kernel(tc, x_words, x_scales, wq_words, wq_scales, wk_
         plane_q1 = keep.tile([P, PASSES, 3 * BLOCK], U8, align_bytes=64, name="plane_q1")
         plane_k = keep.tile([P, PASSES, 4 * BLOCK], U8, align_bytes=64, name="plane_k")
         w_codes = []
-        for b in range(1, 8):
-            wt = keep.tile([P, PASSES, 2 * BLOCK], U8, align_bytes=64, name="w_block%d" % b)
+        for b in (1, 2, 4, 6):
+            wt = keep.tile([P, PASSES, (2 if b == 1 else 4) * BLOCK], U8, align_bytes=64, name="w_block%d" % b)
             w_codes.append(wt)
 
         zeros = keep.tile([P, BLOCK], BF16, align_bytes=64, name="zeros")
@@ -68,9 +68,9 @@ def tile_selfattention_pa_kernel(tc, x_words, x_scales, wq_words, wq_scales, wk_
         def x_src(g0, n):
             return x_words[g0 : g0 + n, :, :].rearrange("g p n -> p g n")
 
-        def w_src(b, g0, n):
+        def w_src(b, g0, n, blocks=1):
             c0 = (b % 4) * 2 * BLOCK
-            return words[b // 4][g0 : g0 + n, :, c0 : c0 + 2 * BLOCK].rearrange("g p n -> p g n")
+            return words[b // 4][g0 : g0 + n, :, c0 : c0 + blocks * 2 * BLOCK].rearrange("g p n -> p g n")
 
         nc.sync.dma_start(out=w_first[:], in_=w_src(0, 0, 1))
         nc.sync.dma_start(out=x_first[:], in_=x_src(0, 1))
@@ -82,11 +82,10 @@ def tile_selfattention_pa_kernel(tc, x_words, x_scales, wq_words, wq_scales, wk_
         nc.sync.dma_start(out=x_last[:], in_=x_src(3, 3))
         nc.sync.dma_start(out=w_codes[0][:], in_=w_src(1, 0, 6))
         load_planes(plane_q1, scales[0], BLOCK, 3 * BLOCK)
-        nc.sync.dma_start(out=w_codes[1][:], in_=w_src(2, 0, 6))
-        nc.sync.dma_start(out=w_codes[2][:], in_=w_src(3, 0, 6))
+        nc.sync.dma_start(out=w_codes[1][:], in_=w_src(2, 0, 6, 2))
         load_planes(plane_k, scales[1], 0, 4 * BLOCK)
-        for b in range(4, 8):
-            nc.sync.dma_start(out=w_codes[b - 1][:], in_=w_src(b, 0, 6))
+        for b in (4, 6):
+            nc.sync.dma_start(out=w_codes[b // 2][:], in_=w_src(b, 0, 6, 2))
 
         cos_sb = keep.tile([P, TILES, HALF], BF16, name="cos_sb")
         sin_sb = keep.tile([P, TILES, HALF], BF16, name="sin_sb")
@@ -109,7 +108,8 @@ def tile_selfattention_pa_kernel(tc, x_words, x_scales, wq_words, wq_scales, wk_
             if b == 0:
                 part, i = ((w_first, 0), (w_mid, g - 1), (w_mid, g - 1), (w_last, g - 3), (w_last, g - 3), (w_last, g - 3))[g]
             else:
-                part, i = w_codes[b - 1], g
+                part, i = w_codes[b // 2], g
+                c0 = c0 + (BLOCK if b > 1 and b % 2 else 0)
             return part[:, i, 2 * c0 : 2 * (c0 + width)]
 
         def w_scale(b, g, c0, width):
@@ -137,7 +137,7 @@ def tile_selfattention_pa_kernel(tc, x_words, x_scales, wq_words, wq_scales, wk_
 
         def scale_and_store(state):
             (b, t, c0, width), v, r = state
-            o = work.tile([P, BLOCK], F32, name="o", bufs=8)
+            o = work.tile([P, BLOCK], F32, name="o", bufs=28)
             for h in range(width // HEAD):
                 nc.scalar.activation(out=o[:, h * HEAD : (h + 1) * HEAD], in_=v[:, h * HEAD : (h + 1) * HEAD], func=ACT.Copy, scale=r[:, h : h + 1])
             col = (b % 4) * BLOCK + c0

@@ -16,9 +16,12 @@ HALF = HEAD // 2
 EPS = 1.1920928955078125e-07
 PASSES = FEATURES // 512
 TILES = TOKENS // P
-BLOCK = 512
+BANK = 512
 COLS = HEADS * HEAD
 FLOPS = 2 * TOKENS * FEATURES * 2 * COLS
+
+CHUNKS = ((0, 0, 256), (0, 256, 256), (0, 512, 512), (0, 1024, 1024), (1, 0, 1024), (1, 1024, 1024))
+SPLITS = ((0, 1), (1, 3), (3, 6))
 
 
 def tile_selfattention_pa_kernel(tc, x_words, x_scales, wq_words, wq_scales, wk_words, wk_scales, cos, sin, out_0, out_1):
@@ -29,139 +32,109 @@ def tile_selfattention_pa_kernel(tc, x_words, x_scales, wq_words, wq_scales, wk_
 
     with ExitStack() as ctx:
         keep = ctx.enter_context(tc.tile_pool(name="keep", bufs=1))
-        work = ctx.enter_context(tc.tile_pool(name="work", bufs=4))
+        work = ctx.enter_context(tc.tile_pool(name="work", bufs=8))
         psum = ctx.enter_context(tc.psum_pool(name="psum", bufs=8))
         ctx.enter_context(tc.manual_schedule())
 
-        def load_planes(plane, src, col0, width):
-            for q in range(4):
+        def codes_tile(passes, width, name):
+            return keep.tile([P, passes, 2 * width], U8, align_bytes=64, name=name)
+
+        def plane_tile(width, name):
+            return keep.tile([P, PASSES, width], U8, align_bytes=64, name=name)
+
+        def load_codes(tile, src, g0, g1, col0, width):
+            nc.sync.dma_start(out=tile[:], in_=src[g0:g1, :, 2 * col0 : 2 * (col0 + width)].rearrange("g p n -> p g n"))
+
+        def load_plane(plane, src, col0, width):
+            for r in range(4):
                 nc.sync.dma_start(
-                    out=plane[32 * q : 32 * q + 4, :, :].bitcast(I32),
-                    in_=src[:, 4 * q : 4 * q + 4, col0 : col0 + width].rearrange("g r n -> r g n").bitcast(I32),
+                    out=plane[r:P:32, :, :].bitcast(I32),
+                    in_=src[:, r:16:4, col0 : col0 + width].rearrange("g q n -> q g n").bitcast(I32),
                 )
 
-        def flat32(plane):
-            return plane[:].rearrange("p g n -> p (g n)").bitcast(I32)
+        def fill(engine, plane):
+            engine.memset(plane[:].rearrange("p g n -> p (g n)").bitcast(I32), 0)
 
-        x_first = keep.tile([P, 1, 2 * TOKENS], U8, align_bytes=64, name="x_first")
-        x_mid = keep.tile([P, 2, 2 * TOKENS], U8, align_bytes=64, name="x_mid")
-        x_last = keep.tile([P, 3, 2 * TOKENS], U8, align_bytes=64, name="x_last")
-        w_first = keep.tile([P, 1, 2 * BLOCK], U8, align_bytes=64, name="w_first")
-        w_mid = keep.tile([P, 2, 2 * BLOCK], U8, align_bytes=64, name="w_mid")
-        w_last = keep.tile([P, 3, 2 * BLOCK], U8, align_bytes=64, name="w_last")
-        x_plane = keep.tile([P, PASSES, TOKENS], U8, align_bytes=64, name="x_plane")
-        plane_q0 = keep.tile([P, PASSES, BLOCK], U8, align_bytes=64, name="plane_q0")
-        plane_q1 = keep.tile([P, PASSES, 3 * BLOCK], U8, align_bytes=64, name="plane_q1")
-        plane_k = keep.tile([P, PASSES, 4 * BLOCK], U8, align_bytes=64, name="plane_k")
-        w_codes = []
-        for b in (1, 2, 4, 6):
-            wt = keep.tile([P, PASSES, (2 if b == 1 else 4) * BLOCK], U8, align_bytes=64, name="w_block%d" % b)
-            w_codes.append(wt)
+        x_parts = [codes_tile(g1 - g0, TOKENS, "x_codes%d" % g0) for g0, g1 in SPLITS]
+        a_parts = [codes_tile(g1 - g0, CHUNKS[0][2], "a_codes%d" % g0) for g0, g1 in SPLITS]
+        w_tiles = [None] + [codes_tile(PASSES, width, "w_codes%d" % first) for first, (w, c, width) in enumerate(CHUNKS) if first]
+        x_plane = plane_tile(TOKENS, "x_plane")
+        planes = [plane_tile(width, "w_plane%d" % k) for k, (w, c, width) in enumerate(CHUNKS)]
 
-        zeros = keep.tile([P, BLOCK], BF16, align_bytes=64, name="zeros")
-        nc.vector.memset(zeros[:], 0.0)
-        nc.gpsimd.memset(flat32(x_plane), 0)
-        nc.vector.memset(flat32(plane_q0), 0)
-        nc.vector.memset(flat32(plane_q1), 0)
-        nc.vector.memset(flat32(plane_k), 0)
-
-        def x_src(g0, n):
-            return x_words[g0 : g0 + n, :, :].rearrange("g p n -> p g n")
-
-        def w_src(b, g0, n, blocks=1):
-            c0 = (b % 4) * 2 * BLOCK
-            return words[b // 4][g0 : g0 + n, :, c0 : c0 + blocks * 2 * BLOCK].rearrange("g p n -> p g n")
-
-        nc.sync.dma_start(out=w_first[:], in_=w_src(0, 0, 1))
-        nc.sync.dma_start(out=x_first[:], in_=x_src(0, 1))
-        load_planes(x_plane, x_scales, 0, TOKENS)
-        load_planes(plane_q0, scales[0], 0, BLOCK)
-        nc.sync.dma_start(out=w_mid[:], in_=w_src(0, 1, 2))
-        nc.sync.dma_start(out=x_mid[:], in_=x_src(1, 2))
-        nc.sync.dma_start(out=w_last[:], in_=w_src(0, 3, 3))
-        nc.sync.dma_start(out=x_last[:], in_=x_src(3, 3))
-        nc.sync.dma_start(out=w_codes[0][:], in_=w_src(1, 0, 6))
-        load_planes(plane_q1, scales[0], BLOCK, 3 * BLOCK)
-        nc.sync.dma_start(out=w_codes[1][:], in_=w_src(2, 0, 6, 2))
-        load_planes(plane_k, scales[1], 0, 4 * BLOCK)
-        for b in (4, 6):
-            nc.sync.dma_start(out=w_codes[b // 2][:], in_=w_src(b, 0, 6, 2))
-
+        zeros = keep.tile([P, BANK], BF16, align_bytes=64, name="zeros")
         cos_sb = keep.tile([P, TILES, HALF], BF16, name="cos_sb")
         sin_sb = keep.tile([P, TILES, HALF], BF16, name="sin_sb")
         table = keep.tile([P, TILES, 2, HEAD], BF16, name="table")
         dummy = keep.tile([P, 1], F32, name="dummy")
+        nc.vector.memset(zeros[:], 0.0)
+        fill(nc.gpsimd, x_plane)
         nc.gpsimd.dma_start(out=cos_sb[:], in_=cos.rearrange("a (t p) b j -> p (a t) (b j)", p=P))
         nc.gpsimd.dma_start(out=sin_sb[:], in_=sin.rearrange("a (t p) b j -> p (a t) (b j)", p=P))
+        fill(nc.vector, planes[0])
         nc.vector.memset(dummy[:], 1.0)
+        fill(nc.vector, planes[1])
+        fill(nc.vector, planes[2])
+        fill(nc.vector, planes[3])
+        fill(nc.gpsimd, planes[4])
+        fill(nc.gpsimd, planes[5])
         nc.scalar.activation(out=dummy[:], in_=dummy[:], func=ACT.Abs_reciprocal_sqrt)
         nc.scalar.copy(out=table[:, :, 0, 0:HALF], in_=cos_sb[:])
         nc.scalar.copy(out=table[:, :, 1, HALF:HEAD], in_=cos_sb[:])
         nc.scalar.copy(out=table[:, :, 0, HALF:HEAD], in_=sin_sb[:])
         nc.scalar.activation(out=table[:, :, 1, 0:HALF], in_=sin_sb[:], func=ACT.Copy, scale=-1.0)
 
-        def x_pass(g, t):
-            part, i = ((x_first, 0), (x_mid, g - 1), (x_mid, g - 1), (x_last, g - 3), (x_last, g - 3), (x_last, g - 3))[g]
-            return part[:, i, 2 * P * t : 2 * P * (t + 1)]
+        for s, (g0, g1) in enumerate(SPLITS):
+            load_codes(a_parts[s], words[0], g0, g1, 0, CHUNKS[0][2])
+            load_codes(x_parts[s], x_words, g0, g1, 0, TOKENS)
+            if s == 0:
+                load_plane(x_plane, x_scales, 0, TOKENS)
+                load_plane(planes[0], scales[0], 0, CHUNKS[0][2])
+        for k, (w, c, width) in enumerate(CHUNKS):
+            if k:
+                load_plane(planes[k], scales[w], c, width)
+                load_codes(w_tiles[k], words[w], 0, PASSES, c, width)
 
-        def w_pass(b, g, c0, width):
-            if b == 0:
-                part, i = ((w_first, 0), (w_mid, g - 1), (w_mid, g - 1), (w_last, g - 3), (w_last, g - 3), (w_last, g - 3))[g]
-            else:
-                part, i = w_codes[b // 2], g
-                c0 = c0 + (BLOCK if b > 1 and b % 2 else 0)
-            return part[:, i, 2 * c0 : 2 * (c0 + width)]
+        def by_split(parts, g):
+            s = [g0 <= g < g1 for g0, g1 in SPLITS].index(True)
+            return parts[s][:, g - SPLITS[s][0], :]
 
-        def w_scale(b, g, c0, width):
-            if b == 0:
-                return plane_q0[:, g, c0 : c0 + width]
-            if b < 4:
-                c0 = c0 + (b - 1) * BLOCK
-                return plane_q1[:, g, c0 : c0 + width]
-            c0 = c0 + (b - 4) * BLOCK
-            return plane_k[:, g, c0 : c0 + width]
-
-        def mx(acc, b, t, g, c0, width):
+        def mx(acc, k, t, g, c0, width):
+            w_codes = by_split(a_parts, g) if k == 0 else w_tiles[k][:, g, :]
             nc.tensor.matmul_mx(
                 out=acc[:, 0:width],
-                lhsT=x_pass(g, t).bitcast(FP4X4),
+                lhsT=by_split(x_parts, g)[:, 2 * P * t : 2 * P * (t + 1)].bitcast(FP4X4),
                 lhsT_scale=x_plane[:, g, P * t : P * (t + 1)],
-                rhs=w_pass(b, g, c0, width).bitcast(FP4X4),
-                rhs_scale=w_scale(b, g, c0, width),
+                rhs=w_codes[:, 2 * c0 : 2 * (c0 + width)].bitcast(FP4X4),
+                rhs_scale=planes[k][:, g, c0 : c0 + width],
                 start=(g == 0),
                 stop=(g == PASSES - 1),
             )
 
-        pieces = [(b, t, 0, BLOCK) for b in range(8) for t in range(TILES)]
-        pieces[-2:] = [(7, 1, 0, 256), (7, 1, 256, 256), (7, 2, 0, 256), (7, 2, 256, 128), (7, 2, 384, 128)]
+        pieces = [(k, t, c0, min(width, BANK)) for k, (w, c, width) in enumerate(CHUNKS) for c0 in range(0, width, BANK) for t in range(TILES)]
+        last = len(CHUNKS) - 1
+        pieces[-2:] = [(last, 1, 512, 256), (last, 1, 768, 256), (last, 2, 512, 256), (last, 2, 768, 128), (last, 2, 896, 128)]
+        n = len(pieces)
+        on_vector = {4, 9, 14, 19, 23, 24, n - 2, n - 1}
 
-        def scale_and_store(state):
-            (b, t, c0, width), v, r = state
-            o = work.tile([P, BLOCK], F32, name="o", bufs=28)
-            for h in range(width // HEAD):
-                nc.scalar.activation(out=o[:, h * HEAD : (h + 1) * HEAD], in_=v[:, h * HEAD : (h + 1) * HEAD], func=ACT.Copy, scale=r[:, h : h + 1])
-            col = (b % 4) * BLOCK + c0
-            nc.sync.dma_start(out=outs[b // 4][P * t : P * (t + 1), col : col + width], in_=o[:, 0:width])
-
-        warm = psum.tile([P, BLOCK], F32, name="acc")
+        warm = psum.tile([P, BANK], F32, name="acc")
         for i in range(8):
             nc.tensor.matmul(warm[:], zeros[:, 0:P], zeros[:], start=True, stop=True)
 
-        first = [psum.tile([P, BLOCK], F32, name="acc") for t in range(TILES)]
+        first = [psum.tile([P, BANK], F32, name="acc") for t in range(TILES)]
         for g in range(PASSES):
             for t in range(TILES):
-                mx(first[t], 0, t, g, 0, BLOCK)
+                mx(first[t], 0, t, g, 0, CHUNKS[0][2])
 
         def multiply(i):
-            b, t, c0, width = pieces[i]
+            k, t, c0, width = pieces[i]
             nh = width // HEAD
             if i < TILES:
                 acc = first[i]
             else:
-                acc = psum.tile([P, BLOCK], F32, name="acc")
+                acc = psum.tile([P, BANK], F32, name="acc")
                 for g in range(PASSES):
-                    mx(acc, b, t, g, c0, width)
-            prod = work.tile([P, BLOCK // HEAD, 2, HEAD], F32, name="prod")
+                    mx(acc, k, t, g, c0, width)
+            prod = work.tile([P, BANK // HEAD, 2, HEAD], F32, name="prod", bufs=6)
             nc.vector.tensor_tensor(
                 out=prod[:, 0:nh, :, :],
                 in0=acc[:, 0:width].rearrange("p (h d) -> p h d", d=HEAD).unsqueeze(2).to_broadcast([P, nh, 2, HEAD]),
@@ -172,8 +145,8 @@ def tile_selfattention_pa_kernel(tc, x_words, x_scales, wq_words, wq_scales, wk_
 
         def add(i, prod):
             width = pieces[i][3]
-            v = work.tile([P, BLOCK], F32, name="v")
-            eng = nc.vector if width == HEAD else nc.gpsimd
+            v = work.tile([P, BANK], F32, name="v")
+            eng = nc.vector if i in on_vector else nc.gpsimd
             halves = prod[:, 0 : width // HEAD, :, :].rearrange("p h q d -> p (h q) d")
             eng.tensor_tensor(
                 out=v[:, 0:width].rearrange("p (m j) -> p m j", j=HALF),
@@ -184,27 +157,41 @@ def tile_selfattention_pa_kernel(tc, x_words, x_scales, wq_words, wq_scales, wk_
             return v
 
         def squares(i, v):
-            ss = work.tile([P, BLOCK // HEAD], F32, name="ss")
+            ss = work.tile([P, BANK // HEAD], F32, name="ss")
             for h in range(pieces[i][3] // HEAD):
+                head = v[:, h * HEAD : (h + 1) * HEAD]
                 sq = work.tile([P, HEAD], F32, name="sq")
-                nc.scalar.activation(out=sq[:], in_=v[:, h * HEAD : (h + 1) * HEAD], func=ACT.Square, accum_out=ss[:, h : h + 1])
+                nc.scalar.activation(out=sq[:], in_=head, func=ACT.Square, accum_out=ss[:, h : h + 1])
             return ss
 
         def root(i, ss):
             nh = pieces[i][3] // HEAD
-            r = work.tile([P, BLOCK // HEAD], F32, name="r")
+            r = work.tile([P, BANK // HEAD], F32, name="r")
             nc.scalar.activation(out=r[:, 0:nh], in_=ss[:, 0:nh], func=ACT.Abs_reciprocal_sqrt, scale=1.0 / HEAD, bias=EPS)
             return r
 
-        n = len(pieces)
-        prods, vs, rs = {}, {}, {}
-        for i in range(n + 2):
-            if i < n:
-                prods[i] = multiply(i)
-            if 1 <= i <= n:
-                vs[i - 1] = add(i - 1, prods[i - 1])
-                ss = squares(i - 1, vs[i - 1])
-            if i >= 2:
-                scale_and_store((pieces[i - 2], vs[i - 2], rs[i - 2]))
-            if 1 <= i <= n:
-                rs[i - 1] = root(i - 1, ss)
+        vs, rs = {}, {}
+
+        def scale_and_store(i):
+            k, t, c0, width = pieces[i]
+            w, c, chunk_width = CHUNKS[k]
+            o = work.tile([P, BANK], F32, name="o", bufs=28)
+            for h in range(width // HEAD):
+                cols = slice(h * HEAD, (h + 1) * HEAD)
+                if i >= n - 2:
+                    nc.vector.tensor_scalar(out=o[:, cols], in0=vs[i][:, cols], scalar1=rs[i][:, h : h + 1], scalar2=None, op0=ALU.mult)
+                else:
+                    nc.scalar.activation(out=o[:, cols], in_=vs[i][:, cols], func=ACT.Copy, scale=rs[i][:, h : h + 1])
+            nc.sync.dma_start(out=outs[w][P * t : P * (t + 1), c + c0 : c + c0 + width], in_=o[:, 0:width])
+
+        def norm(i):
+            ss = squares(i, vs[i])
+            if i > 0:
+                scale_and_store(i - 1)
+            rs[i] = root(i, ss)
+
+        for i in range(n):
+            prod = multiply(i)
+            vs[i] = add(i, prod)
+            norm(i)
+        scale_and_store(n - 1)

@@ -112,9 +112,10 @@ def tile_selfattention_pa_kernel(tc, x_words, x_scales, wq_words, wq_scales, wk_
 
         pieces = [(k, t, c0, min(width, BANK)) for k, (w, c, width) in enumerate(CHUNKS) for c0 in range(0, width, BANK) for t in range(TILES)]
         last = len(CHUNKS) - 1
-        pieces[-2:] = [(last, 1, 512, 256), (last, 1, 768, 256), (last, 2, 512, 256), (last, 2, 768, 128), (last, 2, 896, 128)]
+        pieces[-1:] = [(last, 2, 512, 256), (last, 2, 768, 256)]
         n = len(pieces)
-        on_vector = {4, 9, 14, 19, 23, 24, n - 2, n - 1}
+        add_on_vector = [i for i in range(n - 2) if i % 3 == 2 or i == n - 3]
+        scale_on_vector = [i for i in range(6, n) if i % 3 == 1 or i >= n - 4]
 
         warm = psum.tile([P, BANK], F32, name="acc")
         for i in range(8):
@@ -134,11 +135,11 @@ def tile_selfattention_pa_kernel(tc, x_words, x_scales, wq_words, wq_scales, wk_
                 acc = psum.tile([P, BANK], F32, name="acc")
                 for g in range(PASSES):
                     mx(acc, k, t, g, c0, width)
-            prod = work.tile([P, BANK // HEAD, 2, HEAD], F32, name="prod", bufs=6)
+            prod = work.tile([P, 2, BANK], F32, name="prod", bufs=6)
             nc.vector.tensor_tensor(
-                out=prod[:, 0:nh, :, :],
-                in0=acc[:, 0:width].rearrange("p (h d) -> p h d", d=HEAD).unsqueeze(2).to_broadcast([P, nh, 2, HEAD]),
-                in1=table[:, t, :, :].unsqueeze(1).to_broadcast([P, nh, 2, HEAD]),
+                out=prod[:, :, 0:width].rearrange("p s (h q j) -> p h q s j", q=2, j=HALF),
+                in0=acc[:, 0:width].rearrange("p (h s j) -> p h s j", s=2, j=HALF).unsqueeze(2).to_broadcast([P, nh, 2, 2, HALF]),
+                in1=table[:, t, :, :].rearrange("p q (s j) -> p q s j", s=2).unsqueeze(1).to_broadcast([P, nh, 2, 2, HALF]),
                 op=ALU.mult,
             )
             return prod
@@ -146,14 +147,8 @@ def tile_selfattention_pa_kernel(tc, x_words, x_scales, wq_words, wq_scales, wk_
         def add(i, prod):
             width = pieces[i][3]
             v = work.tile([P, BANK], F32, name="v")
-            eng = nc.vector if i in on_vector else nc.gpsimd
-            halves = prod[:, 0 : width // HEAD, :, :].rearrange("p h q d -> p (h q) d")
-            eng.tensor_tensor(
-                out=v[:, 0:width].rearrange("p (m j) -> p m j", j=HALF),
-                in0=halves[:, :, 0:HALF],
-                in1=halves[:, :, HALF:HEAD],
-                op=ALU.add,
-            )
+            eng = nc.vector if i in add_on_vector else nc.gpsimd
+            eng.tensor_tensor(out=v[:, 0:width], in0=prod[:, 0, 0:width], in1=prod[:, 1, 0:width], op=ALU.add)
             return v
 
         def squares(i, v):
@@ -175,23 +170,34 @@ def tile_selfattention_pa_kernel(tc, x_words, x_scales, wq_words, wq_scales, wk_
         def scale_and_store(i):
             k, t, c0, width = pieces[i]
             w, c, chunk_width = CHUNKS[k]
+            nh = width // HEAD
             o = work.tile([P, BANK], F32, name="o", bufs=28)
-            for h in range(width // HEAD):
-                cols = slice(h * HEAD, (h + 1) * HEAD)
-                if i >= n - 2:
-                    nc.vector.tensor_scalar(out=o[:, cols], in0=vs[i][:, cols], scalar1=rs[i][:, h : h + 1], scalar2=None, op0=ALU.mult)
-                else:
+            if i in scale_on_vector:
+                nc.vector.tensor_tensor(
+                    out=o[:, 0:width].rearrange("p (h d) -> p h d", d=HEAD),
+                    in0=vs[i][:, 0:width].rearrange("p (h d) -> p h d", d=HEAD),
+                    in1=rs[i][:, 0:nh].unsqueeze(2).to_broadcast([P, nh, HEAD]),
+                    op=ALU.mult,
+                )
+            else:
+                for h in range(nh):
+                    cols = slice(h * HEAD, (h + 1) * HEAD)
                     nc.scalar.activation(out=o[:, cols], in_=vs[i][:, cols], func=ACT.Copy, scale=rs[i][:, h : h + 1])
             nc.sync.dma_start(out=outs[w][P * t : P * (t + 1), c + c0 : c + c0 + width], in_=o[:, 0:width])
 
-        def norm(i):
-            ss = squares(i, vs[i])
-            if i > 0:
-                scale_and_store(i - 1)
-            rs[i] = root(i, ss)
-
-        for i in range(n):
-            prod = multiply(i)
-            vs[i] = add(i, prod)
-            norm(i)
-        scale_and_store(n - 1)
+        prods = {}
+        for j in range(n + 3):
+            if j < n:
+                prods[j] = multiply(j)
+            if j - 3 in scale_on_vector:
+                scale_and_store(j - 3)
+            if j < n and j not in add_on_vector:
+                vs[j] = add(j, prods[j])
+            if j - 1 in add_on_vector:
+                vs[j - 1] = add(j - 1, prods[j - 1])
+            if 1 <= j <= n:
+                ss = squares(j - 1, vs[j - 1])
+            if 2 <= j <= n + 1 and j - 2 not in scale_on_vector:
+                scale_and_store(j - 2)
+            if 1 <= j <= n:
+                rs[j - 1] = root(j - 1, ss)

from contextlib import ExitStack

import concourse.mybir as mybir

F32 = mybir.dt.float32
BF16 = mybir.dt.bfloat16
I32 = mybir.dt.int32
U8 = mybir.dt.uint8
FP4X4 = mybir.dt.float4_e2m1fn_x4
ACT = mybir.ActivationFunctionType
ALU = mybir.AluOpType

P = 128
TOKENS, FEATURES, HEADS, HEAD = 384, 3072, 16, 128
HALF = HEAD // 2
EPS = 1.1920928955078125e-07
PASSES = FEATURES // 512
TILES = TOKENS // P
BANK = 512
COLS = HEADS * HEAD
FLOPS = 2 * TOKENS * FEATURES * 2 * COLS

CHUNKS = ((0, 0, 256), (0, 256, 256), (0, 512, 512), (0, 1024, 1024), (1, 0, 1024), (1, 1024, 1024))
SPLITS = ((0, 1), (1, 3), (3, 6))


def tile_selfattention_pa_kernel(tc, x_words, x_scales, wq_words, wq_scales, wk_words, wk_scales, cos, sin, out_0, out_1):
    nc = tc.nc
    outs = [o.rearrange("b t h d -> (b t) (h d)") for o in (out_0, out_1)]
    words = (wq_words, wk_words)
    scales = (wq_scales, wk_scales)

    with ExitStack() as ctx:
        keep = ctx.enter_context(tc.tile_pool(name="keep", bufs=1))
        work = ctx.enter_context(tc.tile_pool(name="work", bufs=8))
        psum = ctx.enter_context(tc.psum_pool(name="psum", bufs=8))
        ctx.enter_context(tc.manual_schedule())

        def codes_tile(passes, width, name):
            return keep.tile([P, passes, 2 * width], U8, align_bytes=64, name=name)

        def plane_tile(width, name):
            return keep.tile([P, PASSES, width], U8, align_bytes=64, name=name)

        def load_codes(tile, src, g0, g1, col0, width):
            nc.sync.dma_start(out=tile[:], in_=src[g0:g1, :, 2 * col0 : 2 * (col0 + width)].rearrange("g p n -> p g n"))

        def load_plane(plane, src, col0, width):
            for r in range(4):
                nc.sync.dma_start(
                    out=plane[r:P:32, :, :].bitcast(I32),
                    in_=src[:, r:16:4, col0 : col0 + width].rearrange("g q n -> q g n").bitcast(I32),
                )

        def fill(engine, plane):
            engine.memset(plane[:].rearrange("p g n -> p (g n)").bitcast(I32), 0)

        x_parts = [codes_tile(g1 - g0, TOKENS, "x_codes%d" % g0) for g0, g1 in SPLITS]
        a_parts = [codes_tile(g1 - g0, CHUNKS[0][2], "a_codes%d" % g0) for g0, g1 in SPLITS]
        w_tiles = [None] + [codes_tile(PASSES, width, "w_codes%d" % first) for first, (w, c, width) in enumerate(CHUNKS) if first]
        x_plane = plane_tile(TOKENS, "x_plane")
        planes = [plane_tile(width, "w_plane%d" % k) for k, (w, c, width) in enumerate(CHUNKS)]

        zeros = keep.tile([P, BANK], BF16, align_bytes=64, name="zeros")
        cos_sb = keep.tile([P, TILES, HALF], BF16, name="cos_sb")
        sin_sb = keep.tile([P, TILES, HALF], BF16, name="sin_sb")
        table = keep.tile([P, TILES, 2, HEAD], BF16, name="table")
        dummy = keep.tile([P, 1], F32, name="dummy")
        nc.vector.memset(zeros[:], 0.0)
        fill(nc.gpsimd, x_plane)
        nc.gpsimd.dma_start(out=cos_sb[:], in_=cos.rearrange("a (t p) b j -> p (a t) (b j)", p=P))
        nc.gpsimd.dma_start(out=sin_sb[:], in_=sin.rearrange("a (t p) b j -> p (a t) (b j)", p=P))
        fill(nc.vector, planes[0])
        nc.vector.memset(dummy[:], 1.0)
        fill(nc.vector, planes[1])
        fill(nc.vector, planes[2])
        fill(nc.vector, planes[3])
        fill(nc.gpsimd, planes[4])
        fill(nc.gpsimd, planes[5])
        nc.scalar.activation(out=dummy[:], in_=dummy[:], func=ACT.Abs_reciprocal_sqrt)
        nc.scalar.copy(out=table[:, :, 0, 0:HALF], in_=cos_sb[:])
        nc.scalar.copy(out=table[:, :, 1, HALF:HEAD], in_=cos_sb[:])
        nc.scalar.copy(out=table[:, :, 0, HALF:HEAD], in_=sin_sb[:])
        nc.scalar.activation(out=table[:, :, 1, 0:HALF], in_=sin_sb[:], func=ACT.Copy, scale=-1.0)

        for s, (g0, g1) in enumerate(SPLITS):
            load_codes(a_parts[s], words[0], g0, g1, 0, CHUNKS[0][2])
            load_codes(x_parts[s], x_words, g0, g1, 0, TOKENS)
            if s == 0:
                load_plane(x_plane, x_scales, 0, TOKENS)
                load_plane(planes[0], scales[0], 0, CHUNKS[0][2])
        for k, (w, c, width) in enumerate(CHUNKS):
            if k:
                load_plane(planes[k], scales[w], c, width)
                load_codes(w_tiles[k], words[w], 0, PASSES, c, width)

        def by_split(parts, g):
            s = [g0 <= g < g1 for g0, g1 in SPLITS].index(True)
            return parts[s][:, g - SPLITS[s][0], :]

        def mx(acc, k, t, g, c0, width):
            w_codes = by_split(a_parts, g) if k == 0 else w_tiles[k][:, g, :]
            nc.tensor.matmul_mx(
                out=acc[:, 0:width],
                lhsT=by_split(x_parts, g)[:, 2 * P * t : 2 * P * (t + 1)].bitcast(FP4X4),
                lhsT_scale=x_plane[:, g, P * t : P * (t + 1)],
                rhs=w_codes[:, 2 * c0 : 2 * (c0 + width)].bitcast(FP4X4),
                rhs_scale=planes[k][:, g, c0 : c0 + width],
                start=(g == 0),
                stop=(g == PASSES - 1),
            )

        pieces = [(k, t, c0, min(width, BANK)) for k, (w, c, width) in enumerate(CHUNKS) for c0 in range(0, width, BANK) for t in range(TILES)]
        last = len(CHUNKS) - 1
        pieces[-1:] = [(last, 2, 512, 256), (last, 2, 768, 256)]
        n = len(pieces)
        add_on_vector = [i for i in range(n - 2) if i % 3 == 2 or i == n - 3]
        scale_on_vector = [i for i in range(6, n) if i % 3 == 1 or i >= n - 4]

        warm = psum.tile([P, BANK], F32, name="acc")
        for i in range(8):
            nc.tensor.matmul(warm[:], zeros[:, 0:P], zeros[:], start=True, stop=True)

        first = [psum.tile([P, BANK], F32, name="acc") for t in range(TILES)]
        for g in range(PASSES):
            for t in range(TILES):
                mx(first[t], 0, t, g, 0, CHUNKS[0][2])

        def multiply(i):
            k, t, c0, width = pieces[i]
            nh = width // HEAD
            if i < TILES:
                acc = first[i]
            else:
                acc = psum.tile([P, BANK], F32, name="acc")
                for g in range(PASSES):
                    mx(acc, k, t, g, c0, width)
            prod = work.tile([P, 2, BANK], F32, name="prod", bufs=6)
            nc.vector.tensor_tensor(
                out=prod[:, :, 0:width].rearrange("p s (h q j) -> p h q s j", q=2, j=HALF),
                in0=acc[:, 0:width].rearrange("p (h s j) -> p h s j", s=2, j=HALF).unsqueeze(2).to_broadcast([P, nh, 2, 2, HALF]),
                in1=table[:, t, :, :].rearrange("p q (s j) -> p q s j", s=2).unsqueeze(1).to_broadcast([P, nh, 2, 2, HALF]),
                op=ALU.mult,
            )
            return prod

        def add(i, prod):
            width = pieces[i][3]
            v = work.tile([P, BANK], F32, name="v")
            eng = nc.vector if i in add_on_vector else nc.gpsimd
            eng.tensor_tensor(out=v[:, 0:width], in0=prod[:, 0, 0:width], in1=prod[:, 1, 0:width], op=ALU.add)
            return v

        def squares(i, v):
            ss = work.tile([P, BANK // HEAD], F32, name="ss")
            for h in range(pieces[i][3] // HEAD):
                head = v[:, h * HEAD : (h + 1) * HEAD]
                sq = work.tile([P, HEAD], F32, name="sq")
                nc.scalar.activation(out=sq[:], in_=head, func=ACT.Square, accum_out=ss[:, h : h + 1])
            return ss

        def root(i, ss):
            nh = pieces[i][3] // HEAD
            r = work.tile([P, BANK // HEAD], F32, name="r")
            nc.scalar.activation(out=r[:, 0:nh], in_=ss[:, 0:nh], func=ACT.Abs_reciprocal_sqrt, scale=1.0 / HEAD, bias=EPS)
            return r

        vs, rs = {}, {}

        def scale_and_store(i):
            k, t, c0, width = pieces[i]
            w, c, chunk_width = CHUNKS[k]
            nh = width // HEAD
            o = work.tile([P, BANK], F32, name="o", bufs=28)
            if i in scale_on_vector:
                nc.vector.tensor_tensor(
                    out=o[:, 0:width].rearrange("p (h d) -> p h d", d=HEAD),
                    in0=vs[i][:, 0:width].rearrange("p (h d) -> p h d", d=HEAD),
                    in1=rs[i][:, 0:nh].unsqueeze(2).to_broadcast([P, nh, HEAD]),
                    op=ALU.mult,
                )
            else:
                for h in range(nh):
                    cols = slice(h * HEAD, (h + 1) * HEAD)
                    nc.scalar.activation(out=o[:, cols], in_=vs[i][:, cols], func=ACT.Copy, scale=rs[i][:, h : h + 1])
            nc.sync.dma_start(out=outs[w][P * t : P * (t + 1), c + c0 : c + c0 + width], in_=o[:, 0:width])

        prods = {}
        for j in range(n + 3):
            if j < n:
                prods[j] = multiply(j)
            if j - 3 in scale_on_vector:
                scale_and_store(j - 3)
            if j < n and j not in add_on_vector:
                vs[j] = add(j, prods[j])
            if j - 1 in add_on_vector:
                vs[j - 1] = add(j - 1, prods[j - 1])
            if 1 <= j <= n:
                ss = squares(j - 1, vs[j - 1])
            if 2 <= j <= n + 1 and j - 2 not in scale_on_vector:
                scale_and_store(j - 2)
            if 1 <= j <= n:
                rs[j - 1] = root(j - 1, ss)
